import numpy as np
import ml_dtypes


def mxq(x, axis, fmt="e4m3"):
    dtype, down = {"e4m3": (ml_dtypes.float8_e4m3fn, 7), "e5m2": (ml_dtypes.float8_e5m2, 14)}[fmt]
    v = np.moveaxis(np.asarray(x, np.float32).astype(ml_dtypes.bfloat16).astype(np.float64), axis, -1)
    blocks = v.reshape(v.shape[:-1] + (-1, 32))
    amax = np.abs(blocks).max(-1, keepdims=True)
    byte = np.maximum(np.where(amax > 0, np.frexp(amax)[1] - 1 + 127, 0) - down, 1)
    scale = np.exp2(byte - 127.0)
    codes = (blocks / scale).astype(np.float32).astype(dtype).astype(np.float64)
    return np.moveaxis((codes * scale).reshape(v.shape), -1, axis)


WIDE = False


def mx_kscale(k):
    if not WIDE:
        return np.ones(k)
    levels = np.array([10, -10, 5, -5, 0])
    a = np.random.permutation(np.resize(levels, k // 512 * 4)).reshape(k // 512, 4)
    idx = np.arange(k)
    return np.exp2(a[idx // 512, idx % 128 // 32])


BF16 = ml_dtypes.bfloat16


def bf(x):
    return np.asarray(x, np.float32).astype(BF16)


def f64(x):
    return np.asarray(x).astype(np.float64)


B, S, E, H, DK = 2, 256, 2048, 16, 128
HD = H * DK


def rotate_half(u):
    shp = u.shape
    u = u.reshape(shp[:-1] + (shp[-1] // 2, 2))
    u1, u2 = u[..., 0], u[..., 1]
    return np.stack((-u2, u1), axis=-1).reshape(shp)


def setup_inputs():
    s = mx_kscale(E)
    theta = np.repeat(np.random.uniform(-np.pi, np.pi, (S, DK // 2)), 2, axis=-1)
    return {"x": bf(np.random.standard_normal((B, S, E)) * s),
            "wq": bf(np.random.standard_normal((HD, E)) / np.sqrt(E) / s[None, :]),
            "wk": bf(np.random.standard_normal((HD, E)) / np.sqrt(E) / s[None, :]),
            "cos_tab": bf(np.cos(theta)),
            "sin_tab": bf(np.sin(theta))}


def reference(x, wq, wk, cos_tab, sin_tab):
    xq = mxq(f64(x), 2, "e4m3")
    c, sn = f64(cos_tab), f64(sin_tab)

    def proj(w):
        y = xq @ mxq(f64(w), 1, "e4m3").T
        return y.reshape(B, S, H, DK).transpose(0, 2, 1, 3)

    def rot(u):
        return u * c + rotate_half(u) * sn

    return rot(proj(wq)), rot(proj(wk))

@@ -1,0 +1,163 @@
+from contextlib import ExitStack
+
+import concourse.mybir as mybir
+from concourse.masks import make_identity
+
+F32 = mybir.dt.float32
+BF16 = mybir.dt.bfloat16
+U32 = mybir.dt.uint32
+U8 = mybir.dt.uint8
+FP8X4 = mybir.dt.float8_e4m3fn_x4
+MULT = mybir.AluOpType.mult
+ADD = mybir.AluOpType.add
+
+P = 128
+B, S, E, H, DK = 2, 256, 2048, 16, 128
+PAIRS = DK // 2
+K_PASS = 4 * P
+PASSES = E // K_PASS
+SLAB = 2 * P
+SLAB_HEADS = SLAB // DK
+W_SLABS = H * DK // SLAB
+N_SLABS = B + 2 * W_SLABS
+
+RAW_BUFS = 8
+LEAD = 2
+
+FLOPS = 2 * B * S * E * 2 * H * DK
+
+
+def tile_multiheadattention_pa_kernel(tc, x, wq, wk, cos_tab, sin_tab, out_0, out_1):
+    nc = tc.nc
+
+    slab_rows = [x[b] for b in range(B)]
+    for w in (wq, wk):
+        slab_rows.extend(w[SLAB * i : SLAB * (i + 1), :] for i in range(W_SLABS))
+
+    with ExitStack() as ctx:
+        const = ctx.enter_context(tc.tile_pool(name="const", bufs=1))
+        raw_pool = ctx.enter_context(tc.tile_pool(name="raw", bufs=RAW_BUFS))
+        mx_pool = ctx.enter_context(tc.tile_pool(name="mx", bufs=LEAD + 1))
+        rot_pool = ctx.enter_context(tc.tile_pool(name="rot", bufs=4))
+        t_psum = ctx.enter_context(tc.psum_pool(name="t_psum", bufs=4))
+        u_psum = ctx.enter_context(tc.psum_pool(name="u_psum", bufs=4))
+        ctx.enter_context(tc.manual_schedule())
+
+        raw = {}
+        grouped = {}
+        codes = {}
+        scales = {}
+
+        def load(n):
+            raw[n] = raw_pool.tile([P, 2, E], BF16, name="raw", tag="raw")
+            nc.sync.dma_start(out=raw[n][:], in_=slab_rows[n].rearrange("(p r) k -> p r k", r=2))
+
+        def transpose(n):
+            h = 1 if n < B else SLAB_HEADS
+            grouped[n] = mx_pool.tile(
+                [P, PASSES * SLAB * 4], BF16, name="grouped", tag="grouped", align_bytes=64
+            )
+            words = grouped[n][:].bitcast(F32).rearrange(
+                "p (g h r i u) -> p g h r i u", g=PASSES, h=h, r=2, u=2
+            )
+            for g0 in range(0, PASSES, 2):
+                for r in range(2):
+                    row_tile = raw[n][:, r, :].bitcast(F32)
+                    bank = t_psum.tile([P, 2, 2, P], F32, name="t_bank", tag="t_bank")
+                    for g in range(2):
+                        for u in range(2):
+                            first = P * (2 * (g0 + g) + u)
+                            nc.tensor.transpose(
+                                bank[:, g, u, :], row_tile[:, first : first + P], identity[:]
+                            )
+                    nc.scalar.copy(
+                        out=words[:, g0 : g0 + 2, :, r, :, :],
+                        in_=bank[:].rearrange("p g u (h i) -> p g h i u", h=h),
+                    )
+
+        def quantise(n):
+            if n < B:
+                codes[n] = const.tile([P, PASSES, SLAB], U32, name="x_codes%d" % n, align_bytes=64)
+                scales[n] = const.tile([P, PASSES, SLAB], U8, name="x_scales%d" % n, align_bytes=64)
+            else:
+                codes[n] = mx_pool.tile([P, PASSES, SLAB], U32, name="codes", tag="codes", align_bytes=64)
+                scales[n] = mx_pool.tile([P, PASSES, SLAB], U8, name="scales", tag="scales", align_bytes=64)
+            half = PASSES // 2
+            for g0 in range(0, PASSES, half):
+                nc.vector.quantize_mx(
+                    out=codes[n][:, g0 : g0 + half, :].rearrange("p g c -> p (g c)").bitcast(FP8X4),
+                    scales=scales[n][:, g0 : g0 + half, :].rearrange("p g c -> p (g c)"),
+                    in_=grouped[n][:, 4 * SLAB * g0 : 4 * SLAB * (g0 + half)],
+                )
+
+        def multiply_and_rotate(s):
+            n = B + s
+            out = out_0 if s < W_SLABS else out_1
+            head = SLAB_HEADS * (s % W_SLABS)
+            for b in range(B):
+                u_bank = u_psum.tile([P, 2, SLAB], F32, name="u_bank", tag="u_bank")
+                for j in range(2):
+                    for g in range(PASSES):
+                        nc.tensor.matmul_mx(
+                            out=u_bank[:, j, :],
+                            lhsT=codes[b][:, g, P * j : P * (j + 1)].bitcast(FP8X4),
+                            lhsT_scale=scales[b][:, g, P * j : P * (j + 1)],
+                            rhs=codes[n][:, g, :].bitcast(FP8X4),
+                            rhs_scale=scales[n][:, g, :],
+                            start=(g == 0),
+                            stop=(g == PASSES - 1),
+                        )
+                members = u_bank[:].rearrange("p j (h r i) -> p (j h) r i", r=2, i=PAIRS)
+                shape = [P, 2 * SLAB_HEADS, 2, PAIRS]
+                a_part = rot_pool.tile(shape, F32, name="a_part", tag="a_part")
+                nc.vector.tensor_tensor(
+                    out=a_part[:], in0=members[:, :, 0:1, :].to_broadcast(shape), in1=table_a, op=MULT
+                )
+                b_part = rot_pool.tile(shape, F32, name="b_part", tag="b_part")
+                nc.vector.tensor_tensor(
+                    out=b_part[:], in0=members[:, :, 1:2, :].to_broadcast(shape), in1=table_b, op=MULT
+                )
+                rotated = rot_pool.tile([P, SLAB_HEADS, 2, PAIRS, 2], F32, name="rotated", tag="rotated")
+                nc.gpsimd.tensor_tensor(
+                    out=rotated[:].rearrange("p h j i r -> p j h i r"),
+                    in0=a_part[:].rearrange("p (j h) r i -> p j h i r", j=2),
+                    in1=b_part[:].rearrange("p (j h) r i -> p j h i r", j=2),
+                    op=ADD,
+                )
+                nc.sync.dma_start(
+                    out=out[b, head : head + SLAB_HEADS].rearrange("h (p j) d -> p h (j d)", j=2),
+                    in_=rotated[:].rearrange("p h j i r -> p h (j i r)"),
+                )
+
+        for n in range(RAW_BUFS):
+            load(n)
+
+        identity = const.tile([P, P], F32, name="identity")
+        make_identity(nc, identity[:])
+
+        cos_sb = const.tile([P, 2, DK], BF16, name="cos_sb")
+        sin_sb = const.tile([P, 2, DK], BF16, name="sin_sb")
+        nc.scalar.dma_start(out=cos_sb[:], in_=cos_tab.rearrange("(p j) d -> p j d", j=2))
+        nc.scalar.dma_start(out=sin_sb[:], in_=sin_tab.rearrange("(p j) d -> p j d", j=2))
+        cos_ri = cos_sb[:].rearrange("p j (i r) -> p j r i", r=2)
+        sin_ri = sin_sb[:].rearrange("p j (i r) -> p j r i", r=2)
+        tab_a = const.tile([P, 2, SLAB_HEADS, 2, PAIRS], F32, name="tab_a")
+        tab_b = const.tile([P, 2, SLAB_HEADS, 2, PAIRS], F32, name="tab_b")
+        for h in range(SLAB_HEADS):
+            nc.vector.tensor_copy(out=tab_a[:, :, h, 0, :], in_=cos_ri[:, :, 0, :])
+            nc.vector.tensor_copy(out=tab_a[:, :, h, 1, :], in_=sin_ri[:, :, 1, :])
+            nc.vector.tensor_scalar_mul(out=tab_b[:, :, h, 0, :], in0=sin_ri[:, :, 0, :], scalar1=-1.0)
+            nc.vector.tensor_copy(out=tab_b[:, :, h, 1, :], in_=cos_ri[:, :, 1, :])
+        table_a = tab_a[:].rearrange("p j h r i -> p (j h) r i")
+        table_b = tab_b[:].rearrange("p j h r i -> p (j h) r i")
+
+        for s in range(-(B + LEAD), 2 * W_SLABS):
+            t = s + B + LEAD
+            if t < N_SLABS:
+                transpose(t)
+                if t + RAW_BUFS < N_SLABS:
+                    load(t + RAW_BUFS)
+            if 0 <= t - 1 < N_SLABS:
+                quantise(t - 1)
+            if s >= 0:
+                multiply_and_rotate(s)

@@ -108,25 +108,31 @@ def tile_multiheadattention_pa_kernel(tc, x, wq, wk, cos_tab, sin_tab, out_0, ou
                             stop=(g == PASSES - 1),
                         )
                 members = u_bank[:].rearrange("p j (h r i) -> p (j h) r i", r=2, i=PAIRS)
-                shape = [P, 2 * SLAB_HEADS, 2, PAIRS]
+                shape = [P, 2 * SLAB_HEADS, PAIRS, 2]
                 a_part = rot_pool.tile(shape, F32, name="a_part", tag="a_part")
                 nc.vector.tensor_tensor(
-                    out=a_part[:], in0=members[:, :, 0:1, :].to_broadcast(shape), in1=table_a, op=MULT
+                    out=a_part[:],
+                    in0=members[:, :, 0, :].unsqueeze(3).to_broadcast(shape),
+                    in1=table_a,
+                    op=MULT,
                 )
                 b_part = rot_pool.tile(shape, F32, name="b_part", tag="b_part")
                 nc.vector.tensor_tensor(
-                    out=b_part[:], in0=members[:, :, 1:2, :].to_broadcast(shape), in1=table_b, op=MULT
+                    out=b_part[:],
+                    in0=members[:, :, 1, :].unsqueeze(3).to_broadcast(shape),
+                    in1=table_b,
+                    op=MULT,
                 )
-                rotated = rot_pool.tile([P, SLAB_HEADS, 2, PAIRS, 2], F32, name="rotated", tag="rotated")
+                rotated = rot_pool.tile([P, SLAB_HEADS, 2, DK], F32, name="rotated", tag="rotated")
                 nc.gpsimd.tensor_tensor(
-                    out=rotated[:].rearrange("p h j i r -> p j h i r"),
-                    in0=a_part[:].rearrange("p (j h) r i -> p j h i r", j=2),
-                    in1=b_part[:].rearrange("p (j h) r i -> p j h i r", j=2),
+                    out=rotated[:].rearrange("p h j d -> p j h d"),
+                    in0=a_part[:].rearrange("p (j h) i r -> p j h (i r)", j=2),
+                    in1=b_part[:].rearrange("p (j h) i r -> p j h (i r)", j=2),
                     op=ADD,
                 )
                 nc.sync.dma_start(
                     out=out[b, head : head + SLAB_HEADS].rearrange("h (p j) d -> p h (j d)", j=2),
-                    in_=rotated[:].rearrange("p h j i r -> p h (j i r)"),
+                    in_=rotated[:].rearrange("p h j d -> p h (j d)"),
                 )
 
         for n in range(RAW_BUFS):
@@ -139,17 +145,17 @@ def tile_multiheadattention_pa_kernel(tc, x, wq, wk, cos_tab, sin_tab, out_0, ou
         sin_sb = const.tile([P, 2, DK], BF16, name="sin_sb")
         nc.scalar.dma_start(out=cos_sb[:], in_=cos_tab.rearrange("(p j) d -> p j d", j=2))
         nc.scalar.dma_start(out=sin_sb[:], in_=sin_tab.rearrange("(p j) d -> p j d", j=2))
-        cos_ri = cos_sb[:].rearrange("p j (i r) -> p j r i", r=2)
-        sin_ri = sin_sb[:].rearrange("p j (i r) -> p j r i", r=2)
-        tab_a = const.tile([P, 2, SLAB_HEADS, 2, PAIRS], F32, name="tab_a")
-        tab_b = const.tile([P, 2, SLAB_HEADS, 2, PAIRS], F32, name="tab_b")
+        cos_ir = cos_sb[:].rearrange("p j (i r) -> p j i r", r=2)
+        sin_ir = sin_sb[:].rearrange("p j (i r) -> p j i r", r=2)
+        tab_a = const.tile([P, 2, SLAB_HEADS, PAIRS, 2], F32, name="tab_a")
+        tab_b = const.tile([P, 2, SLAB_HEADS, PAIRS, 2], F32, name="tab_b")
         for h in range(SLAB_HEADS):
-            nc.vector.tensor_copy(out=tab_a[:, :, h, 0, :], in_=cos_ri[:, :, 0, :])
-            nc.vector.tensor_copy(out=tab_a[:, :, h, 1, :], in_=sin_ri[:, :, 1, :])
-            nc.vector.tensor_scalar_mul(out=tab_b[:, :, h, 0, :], in0=sin_ri[:, :, 0, :], scalar1=-1.0)
-            nc.vector.tensor_copy(out=tab_b[:, :, h, 1, :], in_=cos_ri[:, :, 1, :])
-        table_a = tab_a[:].rearrange("p j h r i -> p (j h) r i")
-        table_b = tab_b[:].rearrange("p j h r i -> p (j h) r i")
+            nc.vector.tensor_copy(out=tab_a[:, :, h, :, 0], in_=cos_ir[:, :, :, 0])
+            nc.vector.tensor_copy(out=tab_a[:, :, h, :, 1], in_=sin_ir[:, :, :, 1])
+            nc.vector.tensor_scalar_mul(out=tab_b[:, :, h, :, 0], in0=sin_ir[:, :, :, 0], scalar1=-1.0)
+            nc.vector.tensor_copy(out=tab_b[:, :, h, :, 1], in_=cos_ir[:, :, :, 1])
+        table_a = tab_a[:].rearrange("p j h i r -> p (j h) i r")
+        table_b = tab_b[:].rearrange("p j h i r -> p (j h) i r")
 
         for s in range(-(B + LEAD), 2 * W_SLABS):
             t = s + B + LEAD

@@ -22,7 +22,8 @@ W_SLABS = H * DK // SLAB
 N_SLABS = B + 2 * W_SLABS
 
 RAW_BUFS = 8
-LEAD = 2
+LEAD = 1
+VECTOR_ADDS_EVERY = 2
 
 FLOPS = 2 * B * S * E * 2 * H * DK
 
@@ -37,7 +38,7 @@ def tile_multiheadattention_pa_kernel(tc, x, wq, wk, cos_tab, sin_tab, out_0, ou
     with ExitStack() as ctx:
         const = ctx.enter_context(tc.tile_pool(name="const", bufs=1))
         raw_pool = ctx.enter_context(tc.tile_pool(name="raw", bufs=RAW_BUFS))
-        mx_pool = ctx.enter_context(tc.tile_pool(name="mx", bufs=LEAD + 1))
+        mx_pool = ctx.enter_context(tc.tile_pool(name="mx", bufs=LEAD + 2))
         rot_pool = ctx.enter_context(tc.tile_pool(name="rot", bufs=4))
         t_psum = ctx.enter_context(tc.psum_pool(name="t_psum", bufs=4))
         u_psum = ctx.enter_context(tc.psum_pool(name="u_psum", bufs=4))
@@ -47,6 +48,7 @@ def tile_multiheadattention_pa_kernel(tc, x, wq, wk, cos_tab, sin_tab, out_0, ou
         grouped = {}
         codes = {}
         scales = {}
+        u_bank, a_part, b_part = {}, {}, {}
 
         def load(n):
             raw[n] = raw_pool.tile([P, 2, E], BF16, name="raw", tag="raw")
@@ -75,31 +77,27 @@ def tile_multiheadattention_pa_kernel(tc, x, wq, wk, cos_tab, sin_tab, out_0, ou
                         in_=bank[:].rearrange("p g u (h i) -> p g h i u", h=h),
                     )
 
-        def quantise(n):
-            if n < B:
+        def quantise(n, g0):
+            if g0 == 0 and n < B:
                 codes[n] = const.tile([P, PASSES, SLAB], U32, name="x_codes%d" % n, align_bytes=64)
                 scales[n] = const.tile([P, PASSES, SLAB], U8, name="x_scales%d" % n, align_bytes=64)
-            else:
+            elif g0 == 0:
                 codes[n] = mx_pool.tile([P, PASSES, SLAB], U32, name="codes", tag="codes", align_bytes=64)
                 scales[n] = mx_pool.tile([P, PASSES, SLAB], U8, name="scales", tag="scales", align_bytes=64)
-            half = PASSES // 2
-            for g0 in range(0, PASSES, half):
-                nc.vector.quantize_mx(
-                    out=codes[n][:, g0 : g0 + half, :].rearrange("p g c -> p (g c)").bitcast(FP8X4),
-                    scales=scales[n][:, g0 : g0 + half, :].rearrange("p g c -> p (g c)"),
-                    in_=grouped[n][:, 4 * SLAB * g0 : 4 * SLAB * (g0 + half)],
-                )
+            nc.vector.quantize_mx(
+                out=codes[n][:, g0 : g0 + 2, :].rearrange("p g c -> p (g c)").bitcast(FP8X4),
+                scales=scales[n][:, g0 : g0 + 2, :].rearrange("p g c -> p (g c)"),
+                in_=grouped[n][:, 4 * SLAB * g0 : 4 * SLAB * (g0 + 2)],
+            )
 
-        def multiply_and_rotate(s):
+        def multiply(s):
             n = B + s
-            out = out_0 if s < W_SLABS else out_1
-            head = SLAB_HEADS * (s % W_SLABS)
             for b in range(B):
-                u_bank = u_psum.tile([P, 2, SLAB], F32, name="u_bank", tag="u_bank")
+                u_bank[b] = u_psum.tile([P, 2, SLAB], F32, name="u_bank", tag="u_bank")
                 for j in range(2):
                     for g in range(PASSES):
                         nc.tensor.matmul_mx(
-                            out=u_bank[:, j, :],
+                            out=u_bank[b][:, j, :],
                             lhsT=codes[b][:, g, P * j : P * (j + 1)].bitcast(FP8X4),
                             lhsT_scale=scales[b][:, g, P * j : P * (j + 1)],
                             rhs=codes[n][:, g, :].bitcast(FP8X4),
@@ -107,33 +105,40 @@ def tile_multiheadattention_pa_kernel(tc, x, wq, wk, cos_tab, sin_tab, out_0, ou
                             start=(g == 0),
                             stop=(g == PASSES - 1),
                         )
-                members = u_bank[:].rearrange("p j (h r i) -> p (j h) r i", r=2, i=PAIRS)
-                shape = [P, 2 * SLAB_HEADS, PAIRS, 2]
-                a_part = rot_pool.tile(shape, F32, name="a_part", tag="a_part")
-                nc.vector.tensor_tensor(
-                    out=a_part[:],
-                    in0=members[:, :, 0, :].unsqueeze(3).to_broadcast(shape),
-                    in1=table_a,
-                    op=MULT,
-                )
-                b_part = rot_pool.tile(shape, F32, name="b_part", tag="b_part")
-                nc.vector.tensor_tensor(
-                    out=b_part[:],
-                    in0=members[:, :, 1, :].unsqueeze(3).to_broadcast(shape),
-                    in1=table_b,
-                    op=MULT,
-                )
-                rotated = rot_pool.tile([P, SLAB_HEADS, 2, DK], F32, name="rotated", tag="rotated")
-                nc.gpsimd.tensor_tensor(
-                    out=rotated[:].rearrange("p h j d -> p j h d"),
-                    in0=a_part[:].rearrange("p (j h) i r -> p j h (i r)", j=2),
-                    in1=b_part[:].rearrange("p (j h) i r -> p j h (i r)", j=2),
-                    op=ADD,
-                )
-                nc.sync.dma_start(
-                    out=out[b, head : head + SLAB_HEADS].rearrange("h (p j) d -> p h (j d)", j=2),
-                    in_=rotated[:].rearrange("p h j d -> p h (j d)"),
-                )
+
+        def products(b):
+            shape = [P, 2 * SLAB_HEADS, PAIRS, 2]
+            members = u_bank[b][:].rearrange("p j (h r i) -> p (j h) r i", r=2, i=PAIRS)
+            a_part[b] = rot_pool.tile(shape, F32, name="a_part", tag="a_part")
+            nc.vector.tensor_tensor(
+                out=a_part[b][:],
+                in0=members[:, :, 0, :].unsqueeze(3).to_broadcast(shape),
+                in1=table_a,
+                op=MULT,
+            )
+            b_part[b] = rot_pool.tile(shape, F32, name="b_part", tag="b_part")
+            nc.vector.tensor_tensor(
+                out=b_part[b][:],
+                in0=members[:, :, 1, :].unsqueeze(3).to_broadcast(shape),
+                in1=table_b,
+                op=MULT,
+            )
+
+        def add_and_store(s, b):
+            out = out_0 if s < W_SLABS else out_1
+            head = SLAB_HEADS * (s % W_SLABS)
+            adder = nc.vector if b == 0 and s % VECTOR_ADDS_EVERY == 0 else nc.gpsimd
+            rotated = rot_pool.tile([P, SLAB_HEADS, 2, DK], F32, name="rotated", tag="rotated")
+            adder.tensor_tensor(
+                out=rotated[:].rearrange("p h j d -> p j h d"),
+                in0=a_part[b][:].rearrange("p (j h) i r -> p j h (i r)", j=2),
+                in1=b_part[b][:].rearrange("p (j h) i r -> p j h (i r)", j=2),
+                op=ADD,
+            )
+            nc.sync.dma_start(
+                out=out[b, head : head + SLAB_HEADS].rearrange("h (p j) d -> p h (j d)", j=2),
+                in_=rotated[:].rearrange("p h j d -> p h (j d)"),
+            )
 
         for n in range(RAW_BUFS):
             load(n)
@@ -163,7 +168,13 @@ def tile_multiheadattention_pa_kernel(tc, x, wq, wk, cos_tab, sin_tab, out_0, ou
                 transpose(t)
                 if t + RAW_BUFS < N_SLABS:
                     load(t + RAW_BUFS)
-            if 0 <= t - 1 < N_SLABS:
-                quantise(t - 1)
+                quantise(t, 0)
             if s >= 0:
-                multiply_and_rotate(s)
+                multiply(s)
+                products(0)
+            if t < N_SLABS:
+                quantise(t, 2)
+            if s >= 0:
+                products(1)
+                add_and_store(s, 0)
+                add_and_store(s, 1)

@@ -23,7 +23,6 @@ N_SLABS = B + 2 * W_SLABS
 
 RAW_BUFS = 8
 LEAD = 1
-VECTOR_ADDS_EVERY = 2
 
 FLOPS = 2 * B * S * E * 2 * H * DK
 
@@ -39,7 +38,7 @@ def tile_multiheadattention_pa_kernel(tc, x, wq, wk, cos_tab, sin_tab, out_0, ou
         const = ctx.enter_context(tc.tile_pool(name="const", bufs=1))
         raw_pool = ctx.enter_context(tc.tile_pool(name="raw", bufs=RAW_BUFS))
         mx_pool = ctx.enter_context(tc.tile_pool(name="mx", bufs=LEAD + 2))
-        rot_pool = ctx.enter_context(tc.tile_pool(name="rot", bufs=4))
+        rot_pool = ctx.enter_context(tc.tile_pool(name="rot", bufs=4 * B))
         t_psum = ctx.enter_context(tc.psum_pool(name="t_psum", bufs=4))
         u_psum = ctx.enter_context(tc.psum_pool(name="u_psum", bufs=4))
         ctx.enter_context(tc.manual_schedule())
@@ -48,7 +47,7 @@ def tile_multiheadattention_pa_kernel(tc, x, wq, wk, cos_tab, sin_tab, out_0, ou
         grouped = {}
         codes = {}
         scales = {}
-        u_bank, a_part, b_part = {}, {}, {}
+        u_bank, prod = {}, {}
 
         def load(n):
             raw[n] = raw_pool.tile([P, 2, E], BF16, name="raw", tag="raw")
@@ -107,32 +106,22 @@ def tile_multiheadattention_pa_kernel(tc, x, wq, wk, cos_tab, sin_tab, out_0, ou
                         )
 
         def products(b):
-            shape = [P, 2 * SLAB_HEADS, PAIRS, 2]
-            members = u_bank[b][:].rearrange("p j (h r i) -> p (j h) r i", r=2, i=PAIRS)
-            a_part[b] = rot_pool.tile(shape, F32, name="a_part", tag="a_part")
+            shape = [P, 2 * SLAB_HEADS * 2, PAIRS, 2]
+            sums = u_bank[b][:].rearrange("p j (m i) -> p (j m) i", i=PAIRS)
+            prod[b] = rot_pool.tile(shape, F32, name="prod", tag="prod")
             nc.vector.tensor_tensor(
-                out=a_part[b][:],
-                in0=members[:, :, 0, :].unsqueeze(3).to_broadcast(shape),
-                in1=table_a,
-                op=MULT,
-            )
-            b_part[b] = rot_pool.tile(shape, F32, name="b_part", tag="b_part")
-            nc.vector.tensor_tensor(
-                out=b_part[b][:],
-                in0=members[:, :, 1, :].unsqueeze(3).to_broadcast(shape),
-                in1=table_b,
-                op=MULT,
+                out=prod[b][:], in0=sums.unsqueeze(3).to_broadcast(shape), in1=table, op=MULT
             )
 
         def add_and_store(s, b):
             out = out_0 if s < W_SLABS else out_1
             head = SLAB_HEADS * (s % W_SLABS)
-            adder = nc.vector if b == 0 and s % VECTOR_ADDS_EVERY == 0 else nc.gpsimd
+            parts = prod[b][:].rearrange("p (j h r) i t -> p j h r (i t)", j=2, r=2)
             rotated = rot_pool.tile([P, SLAB_HEADS, 2, DK], F32, name="rotated", tag="rotated")
-            adder.tensor_tensor(
+            nc.gpsimd.tensor_tensor(
                 out=rotated[:].rearrange("p h j d -> p j h d"),
-                in0=a_part[b][:].rearrange("p (j h) i r -> p j h (i r)", j=2),
-                in1=b_part[b][:].rearrange("p (j h) i r -> p j h (i r)", j=2),
+                in0=parts[:, :, :, 0, :],
+                in1=parts[:, :, :, 1, :],
                 op=ADD,
             )
             nc.sync.dma_start(
@@ -150,17 +139,15 @@ def tile_multiheadattention_pa_kernel(tc, x, wq, wk, cos_tab, sin_tab, out_0, ou
         sin_sb = const.tile([P, 2, DK], BF16, name="sin_sb")
         nc.scalar.dma_start(out=cos_sb[:], in_=cos_tab.rearrange("(p j) d -> p j d", j=2))
         nc.scalar.dma_start(out=sin_sb[:], in_=sin_tab.rearrange("(p j) d -> p j d", j=2))
-        cos_ir = cos_sb[:].rearrange("p j (i r) -> p j i r", r=2)
-        sin_ir = sin_sb[:].rearrange("p j (i r) -> p j i r", r=2)
-        tab_a = const.tile([P, 2, SLAB_HEADS, PAIRS, 2], F32, name="tab_a")
-        tab_b = const.tile([P, 2, SLAB_HEADS, PAIRS, 2], F32, name="tab_b")
+        cos_it = cos_sb[:].rearrange("p j (i t) -> p j i t", t=2)
+        sin_it = sin_sb[:].rearrange("p j (i t) -> p j i t", t=2)
+        factors = const.tile([P, 2, SLAB_HEADS, 2, PAIRS, 2], F32, name="factors")
         for h in range(SLAB_HEADS):
-            nc.vector.tensor_copy(out=tab_a[:, :, h, :, 0], in_=cos_ir[:, :, :, 0])
-            nc.vector.tensor_copy(out=tab_a[:, :, h, :, 1], in_=sin_ir[:, :, :, 1])
-            nc.vector.tensor_scalar_mul(out=tab_b[:, :, h, :, 0], in0=sin_ir[:, :, :, 0], scalar1=-1.0)
-            nc.vector.tensor_copy(out=tab_b[:, :, h, :, 1], in_=cos_ir[:, :, :, 1])
-        table_a = tab_a[:].rearrange("p j h i r -> p (j h) i r")
-        table_b = tab_b[:].rearrange("p j h i r -> p (j h) i r")
+            nc.vector.tensor_copy(out=factors[:, :, h, 0, :, 0], in_=cos_it[:, :, :, 0])
+            nc.vector.tensor_copy(out=factors[:, :, h, 0, :, 1], in_=sin_it[:, :, :, 1])
+            nc.vector.tensor_scalar_mul(out=factors[:, :, h, 1, :, 0], in0=sin_it[:, :, :, 0], scalar1=-1.0)
+            nc.vector.tensor_copy(out=factors[:, :, h, 1, :, 1], in_=cos_it[:, :, :, 1])
+        table = factors[:].rearrange("p j h r i t -> p (j h r) i t")
 
         for s in range(-(B + LEAD), 2 * W_SLABS):
             t = s + B + LEAD

from contextlib import ExitStack

import concourse.mybir as mybir
from concourse.masks import make_identity

F32 = mybir.dt.float32
BF16 = mybir.dt.bfloat16
U32 = mybir.dt.uint32
U8 = mybir.dt.uint8
FP8X4 = mybir.dt.float8_e4m3fn_x4
MULT = mybir.AluOpType.mult
ADD = mybir.AluOpType.add

P = 128
B, S, E, H, DK = 2, 256, 2048, 16, 128
PAIRS = DK // 2
K_PASS = 4 * P
PASSES = E // K_PASS
SLAB = 2 * P
SLAB_HEADS = SLAB // DK
W_SLABS = H * DK // SLAB
N_SLABS = B + 2 * W_SLABS

RAW_BUFS = 8
LEAD = 1

FLOPS = 2 * B * S * E * 2 * H * DK


def tile_multiheadattention_pa_kernel(tc, x, wq, wk, cos_tab, sin_tab, out_0, out_1):
    nc = tc.nc

    slab_rows = [x[b] for b in range(B)]
    for w in (wq, wk):
        slab_rows.extend(w[SLAB * i : SLAB * (i + 1), :] for i in range(W_SLABS))

    with ExitStack() as ctx:
        const = ctx.enter_context(tc.tile_pool(name="const", bufs=1))
        raw_pool = ctx.enter_context(tc.tile_pool(name="raw", bufs=RAW_BUFS))
        mx_pool = ctx.enter_context(tc.tile_pool(name="mx", bufs=LEAD + 2))
        rot_pool = ctx.enter_context(tc.tile_pool(name="rot", bufs=4 * B))
        t_psum = ctx.enter_context(tc.psum_pool(name="t_psum", bufs=4))
        u_psum = ctx.enter_context(tc.psum_pool(name="u_psum", bufs=4))
        ctx.enter_context(tc.manual_schedule())

        raw = {}
        grouped = {}
        codes = {}
        scales = {}
        u_bank, prod = {}, {}

        def load(n):
            raw[n] = raw_pool.tile([P, 2, E], BF16, name="raw", tag="raw")
            nc.sync.dma_start(out=raw[n][:], in_=slab_rows[n].rearrange("(p r) k -> p r k", r=2))

        def transpose(n):
            h = 1 if n < B else SLAB_HEADS
            grouped[n] = mx_pool.tile(
                [P, PASSES * SLAB * 4], BF16, name="grouped", tag="grouped", align_bytes=64
            )
            words = grouped[n][:].bitcast(F32).rearrange(
                "p (g h r i u) -> p g h r i u", g=PASSES, h=h, r=2, u=2
            )
            for g0 in range(0, PASSES, 2):
                for r in range(2):
                    row_tile = raw[n][:, r, :].bitcast(F32)
                    bank = t_psum.tile([P, 2, 2, P], F32, name="t_bank", tag="t_bank")
                    for g in range(2):
                        for u in range(2):
                            first = P * (2 * (g0 + g) + u)
                            nc.tensor.transpose(
                                bank[:, g, u, :], row_tile[:, first : first + P], identity[:]
                            )
                    nc.scalar.copy(
                        out=words[:, g0 : g0 + 2, :, r, :, :],
                        in_=bank[:].rearrange("p g u (h i) -> p g h i u", h=h),
                    )

        def quantise(n, g0):
            if g0 == 0 and n < B:
                codes[n] = const.tile([P, PASSES, SLAB], U32, name="x_codes%d" % n, align_bytes=64)
                scales[n] = const.tile([P, PASSES, SLAB], U8, name="x_scales%d" % n, align_bytes=64)
            elif g0 == 0:
                codes[n] = mx_pool.tile([P, PASSES, SLAB], U32, name="codes", tag="codes", align_bytes=64)
                scales[n] = mx_pool.tile([P, PASSES, SLAB], U8, name="scales", tag="scales", align_bytes=64)
            nc.vector.quantize_mx(
                out=codes[n][:, g0 : g0 + 2, :].rearrange("p g c -> p (g c)").bitcast(FP8X4),
                scales=scales[n][:, g0 : g0 + 2, :].rearrange("p g c -> p (g c)"),
                in_=grouped[n][:, 4 * SLAB * g0 : 4 * SLAB * (g0 + 2)],
            )

        def multiply(s):
            n = B + s
            for b in range(B):
                u_bank[b] = u_psum.tile([P, 2, SLAB], F32, name="u_bank", tag="u_bank")
                for j in range(2):
                    for g in range(PASSES):
                        nc.tensor.matmul_mx(
                            out=u_bank[b][:, j, :],
                            lhsT=codes[b][:, g, P * j : P * (j + 1)].bitcast(FP8X4),
                            lhsT_scale=scales[b][:, g, P * j : P * (j + 1)],
                            rhs=codes[n][:, g, :].bitcast(FP8X4),
                            rhs_scale=scales[n][:, g, :],
                            start=(g == 0),
                            stop=(g == PASSES - 1),
                        )

        def products(b):
            shape = [P, 2 * SLAB_HEADS * 2, PAIRS, 2]
            sums = u_bank[b][:].rearrange("p j (m i) -> p (j m) i", i=PAIRS)
            prod[b] = rot_pool.tile(shape, F32, name="prod", tag="prod")
            nc.vector.tensor_tensor(
                out=prod[b][:], in0=sums.unsqueeze(3).to_broadcast(shape), in1=table, op=MULT
            )

        def add_and_store(s, b):
            out = out_0 if s < W_SLABS else out_1
            head = SLAB_HEADS * (s % W_SLABS)
            parts = prod[b][:].rearrange("p (j h r) i t -> p j h r (i t)", j=2, r=2)
            rotated = rot_pool.tile([P, SLAB_HEADS, 2, DK], F32, name="rotated", tag="rotated")
            nc.gpsimd.tensor_tensor(
                out=rotated[:].rearrange("p h j d -> p j h d"),
                in0=parts[:, :, :, 0, :],
                in1=parts[:, :, :, 1, :],
                op=ADD,
            )
            nc.sync.dma_start(
                out=out[b, head : head + SLAB_HEADS].rearrange("h (p j) d -> p h (j d)", j=2),
                in_=rotated[:].rearrange("p h j d -> p h (j d)"),
            )

        for n in range(RAW_BUFS):
            load(n)

        identity = const.tile([P, P], F32, name="identity")
        make_identity(nc, identity[:])

        cos_sb = const.tile([P, 2, DK], BF16, name="cos_sb")
        sin_sb = const.tile([P, 2, DK], BF16, name="sin_sb")
        nc.scalar.dma_start(out=cos_sb[:], in_=cos_tab.rearrange("(p j) d -> p j d", j=2))
        nc.scalar.dma_start(out=sin_sb[:], in_=sin_tab.rearrange("(p j) d -> p j d", j=2))
        cos_it = cos_sb[:].rearrange("p j (i t) -> p j i t", t=2)
        sin_it = sin_sb[:].rearrange("p j (i t) -> p j i t", t=2)
        factors = const.tile([P, 2, SLAB_HEADS, 2, PAIRS, 2], F32, name="factors")
        for h in range(SLAB_HEADS):
            nc.vector.tensor_copy(out=factors[:, :, h, 0, :, 0], in_=cos_it[:, :, :, 0])
            nc.vector.tensor_copy(out=factors[:, :, h, 0, :, 1], in_=sin_it[:, :, :, 1])
            nc.vector.tensor_scalar_mul(out=factors[:, :, h, 1, :, 0], in0=sin_it[:, :, :, 0], scalar1=-1.0)
            nc.vector.tensor_copy(out=factors[:, :, h, 1, :, 1], in_=cos_it[:, :, :, 1])
        table = factors[:].rearrange("p j h r i t -> p (j h r) i t")

        for s in range(-(B + LEAD), 2 * W_SLABS):
            t = s + B + LEAD
            if t < N_SLABS:
                transpose(t)
                if t + RAW_BUFS < N_SLABS:
                    load(t + RAW_BUFS)
                quantise(t, 0)
            if s >= 0:
                multiply(s)
                products(0)
            if t < N_SLABS:
                quantise(t, 2)
            if s >= 0:
                products(1)
                add_and_store(s, 0)
                add_and_store(s, 1)
